import numpy as np
import ml_dtypes


def mxq(x, axis, fmt="e4m3"):
    dtype, down = {"e4m3": (ml_dtypes.float8_e4m3fn, 7), "e5m2": (ml_dtypes.float8_e5m2, 14)}[fmt]
    v = np.moveaxis(np.asarray(x, np.float32).astype(ml_dtypes.bfloat16).astype(np.float64), axis, -1)
    blocks = v.reshape(v.shape[:-1] + (-1, 32))
    amax = np.abs(blocks).max(-1, keepdims=True)
    byte = np.maximum(np.where(amax > 0, np.frexp(amax)[1] - 1 + 127, 0) - down, 1)
    scale = np.exp2(byte - 127.0)
    codes = (blocks / scale).astype(np.float32).astype(dtype).astype(np.float64)
    return np.moveaxis((codes * scale).reshape(v.shape), -1, axis)


WIDE = False


def mx_kscale(k):
    if not WIDE:
        return np.ones(k)
    levels = np.array([10, -10, 5, -5, 0])
    a = np.random.permutation(np.resize(levels, k // 512 * 4)).reshape(k // 512, 4)
    idx = np.arange(k)
    return np.exp2(a[idx // 512, idx % 128 // 32])


BF16 = ml_dtypes.bfloat16


def bf(x):
    return np.asarray(x, np.float32).astype(BF16)


def f64(x):
    return np.asarray(x).astype(np.float64)


B, P0, P1, P2, K0, K1, K2 = 128, 4096, 9216, 7168, 512, 512, 512
PT = P0 + P1 + P2
KT = K0 + K1 + K2
CLIP1 = 1.0


def clip_rows(mat, clip):
    norms = np.sqrt(np.sum(mat * mat, axis=1, keepdims=True))
    scale = np.minimum(clip / norms, 1.0)
    return mat * scale


def setup_inputs():
    t0, t1, t2 = mx_kscale(K0), mx_kscale(K1), mx_kscale(K2)
    r = np.exp2(np.random.uniform(-2.0, 2.0, (B, 1))) / (KT * PT) ** 0.25
    return {"target_grad": bf(np.random.standard_normal((B, PT)) * r),
            "embedding": bf(np.random.standard_normal((B, KT)) * r * np.concatenate([t0, t1, t2])),
            "bases0": bf(np.random.standard_normal((P0, K0)) / np.sqrt(P0) / t0[None, :]),
            "bases1": bf(np.random.standard_normal((P1, K1)) / np.sqrt(P1) / t1[None, :]),
            "bases2": bf(np.random.standard_normal((P2, K2)) / np.sqrt(P2) / t2[None, :])}


def reference(target_grad, embedding, bases0, bases1, bases2):
    g = f64(target_grad)
    e = f64(embedding)
    approx_parts = []
    offset = 0
    for b in (f64(bases0), f64(bases1), f64(bases2)):
        num_k = b.shape[1]
        approx_parts.append(mxq(e[:, offset:offset + num_k], 1, "e4m3") @ mxq(b.T, 0, "e4m3"))
        offset += num_k
    no_reduction_approx = np.concatenate(approx_parts, axis=1)
    residual = g - no_reduction_approx
    return np.sum(clip_rows(residual, CLIP1), axis=0) / B

@@ -1,0 +1,219 @@
+from contextlib import ExitStack
+
+import concourse.mybir as mybir
+from concourse.masks import make_identity
+
+F32 = mybir.dt.float32
+BF16 = mybir.dt.bfloat16
+U32 = mybir.dt.uint32
+U8 = mybir.dt.uint8
+FP8X4 = mybir.dt.float8_e4m3fn_x4
+ALU = mybir.AluOpType
+ACT = mybir.ActivationFunctionType
+
+P = 128
+K = 512
+PACK = 4
+HALVES = 2
+SLOTS = 4
+CHUNK = P * SLOTS
+SLOTS_PER_BANK = 2
+ROUND = 2
+G_ROUNDS = 2
+AHEAD = 3
+WINDOW = 32
+
+FLOPS = 2 * 128 * 20480 * 512
+
+
+def tile_gep_pb_kernel(tc, target_grad, embedding, bases0, bases1, bases2, out):
+    nc = tc.nc
+    groups = (bases0, bases1, bases2)
+    n_groups = len(groups)
+
+    chunk_group = []
+    chunk_rows = []
+    for i, bases in enumerate(groups):
+        for first in range(0, bases.shape[0], CHUNK):
+            chunk_group.append(i)
+            chunk_rows.append(bases[first : first + CHUNK, :])
+    n_rounds = len(chunk_rows) // ROUND
+    round_cols = ROUND * CHUNK
+    n_col_tiles = n_rounds * round_cols // P
+
+    with ExitStack() as stack:
+        keep = stack.enter_context(tc.tile_pool(name="keep", bufs=1))
+        raw_pool = stack.enter_context(tc.tile_pool(name="raw_pool", bufs=(AHEAD + 1) * ROUND))
+        stage = stack.enter_context(tc.tile_pool(name="stage", bufs=2 * ROUND))
+        xt_pool = stack.enter_context(tc.psum_pool(name="xt_pool", bufs=6))
+        acc_pool = stack.enter_context(tc.psum_pool(name="acc_pool", bufs=ROUND))
+        stack.enter_context(tc.manual_schedule())
+
+        ident = keep.tile([P, P], F32, name="ident")
+        e_sb = keep.tile([P, n_groups, K], BF16, name="e_sb")
+        e_grouped = keep.tile([P, n_groups * P * PACK], BF16, name="e_grouped", align_bytes=64)
+        e_codes = keep.tile([P, n_groups, P], U32, name="e_codes", align_bytes=64)
+        e_scales = keep.tile([P, n_groups, P], U8, name="e_scales", align_bytes=64)
+        g_tiles = [
+            keep.tile([P, G_ROUNDS * round_cols], BF16, name="g%d" % q)
+            for q in range(n_rounds // G_ROUNDS)
+        ]
+        r_tiles = [keep.tile([P, round_cols], F32, name="r%d" % n) for n in range(n_rounds)]
+        sq_sums = keep.tile([P, n_rounds], F32, name="sq_sums")
+        one = keep.tile([P, 1], F32, name="one")
+        warm = keep.tile([P, 1], F32, name="warm")
+        norm_sq = keep.tile([P, 1], F32, name="norm_sq")
+        floored = keep.tile([P, 1], F32, name="floored")
+        norm_b = keep.tile([P, 1], F32, name="norm_b")
+        c_window = keep.tile([P, 2 * WINDOW - 1], F32, name="c_window")
+        out_cols = keep.tile([P, 2 * P], F32, name="out_cols")
+        out_rows = keep.tile([P, 2 * P], F32, name="out_rows")
+
+        raw = {}
+        grouped = {}
+        codes = {}
+        scales = {}
+        acc = {}
+
+        def load_round(n):
+            for c in range(n * ROUND, (n + 1) * ROUND):
+                raw[c] = raw_pool.tile([P, SLOTS, K], BF16, name="raw")
+                nc.sync.dma_start(
+                    out=raw[c][:], in_=chunk_rows[c].rearrange("(p t) k -> p t k", t=SLOTS)
+                )
+            if n % G_ROUNDS == 0:
+                q = n // G_ROUNDS
+                width = G_ROUNDS * round_cols
+                nc.sync.dma_start(out=g_tiles[q][:], in_=target_grad[:, q * width : (q + 1) * width])
+
+        def transpose_slots(words, slots):
+            bank = xt_pool.tile([P, SLOTS_PER_BANK, HALVES, P], F32, name="xt")
+            for s, t in enumerate(slots):
+                for u in range(HALVES):
+                    nc.tensor.transpose(bank[:, s, u, :], words[:, t, u * P : (u + 1) * P], ident[:])
+            return bank
+
+        def words_view(tile_ap, slots):
+            return tile_ap.bitcast(F32).rearrange("q (t p u) -> q t p u", t=slots, u=HALVES)
+
+        def bank_source(bank, slots):
+            return bank[:, 0:slots].rearrange("q t u p -> q t p u")
+
+        def transpose_round(n):
+            banks = []
+            for c in range(n * ROUND, (n + 1) * ROUND):
+                words = raw[c][:].bitcast(F32)
+                for first in range(0, SLOTS, SLOTS_PER_BANK):
+                    banks.append((c, first, transpose_slots(words, range(first, first + SLOTS_PER_BANK))))
+            for c in range(n * ROUND, (n + 1) * ROUND):
+                grouped[c] = stage.tile([P, CHUNK * PACK], BF16, name="grouped", align_bytes=64)
+            for b, (c, first, bank) in enumerate(banks):
+                dst = words_view(grouped[c][:], SLOTS)[:, first : first + SLOTS_PER_BANK]
+                if b == len(banks) - 1:
+                    nc.vector.tensor_copy(out=dst, in_=bank_source(bank, SLOTS_PER_BANK))
+                else:
+                    nc.scalar.copy(out=dst, in_=bank_source(bank, SLOTS_PER_BANK))
+
+        def quantise_round(n):
+            for c in range(n * ROUND, (n + 1) * ROUND):
+                codes[c] = stage.tile([P, CHUNK], U32, name="codes", align_bytes=64)
+                scales[c] = stage.tile([P, CHUNK], U8, name="scales", align_bytes=64)
+                nc.vector.quantize_mx(
+                    out=codes[c][:].bitcast(FP8X4), scales=scales[c][:], in_=grouped[c][:]
+                )
+
+        def multiply_round(n):
+            for c in range(n * ROUND, (n + 1) * ROUND):
+                i = chunk_group[c]
+                acc[c] = acc_pool.tile([P, CHUNK], F32, name="acc")
+                nc.tensor.matmul_mx(
+                    out=acc[c][:],
+                    lhsT=e_codes[:, i, :].bitcast(FP8X4),
+                    lhsT_scale=e_scales[:, i, :],
+                    rhs=codes[c][:].bitcast(FP8X4),
+                    rhs_scale=scales[c][:],
+                    start=True,
+                    stop=True,
+                )
+
+        def subtract_round(n):
+            for h in range(ROUND):
+                c = n * ROUND + h
+                g_first = (n % G_ROUNDS) * round_cols + h * CHUNK
+                nc.vector.tensor_tensor(
+                    out=r_tiles[n][:, h * CHUNK : (h + 1) * CHUNK].rearrange("b (p t) -> b p t", t=SLOTS),
+                    in0=g_tiles[n // G_ROUNDS][:, g_first : g_first + CHUNK].rearrange(
+                        "b (p t) -> b p t", t=SLOTS
+                    ),
+                    in1=acc[c][:].rearrange("b (t p) -> b p t", t=SLOTS),
+                    op=ALU.subtract,
+                )
+
+        def square_round(n):
+            squares = stage.tile([P, round_cols], BF16, name="squares")
+            nc.scalar.activation(
+                out=squares[:], in_=r_tiles[n][:], func=ACT.Square, accum_out=sq_sums[:, n : n + 1]
+            )
+
+        nc.sync.dma_start(out=e_sb[:], in_=embedding.rearrange("b (i k) -> b i k", k=K))
+        for n in range(AHEAD):
+            load_round(n)
+        make_identity(nc, ident[:])
+        nc.vector.memset(one[:], 1.0)
+        nc.vector.memset(c_window[:], 0.0)
+        nc.vector.memset(out_cols[:], 0.0)
+        nc.scalar.activation(out=warm[:], in_=one[:], func=ACT.Sqrt)
+
+        e_words = e_sb[:].bitcast(F32)
+        for first in range(0, n_groups, SLOTS_PER_BANK):
+            slots = range(first, min(first + SLOTS_PER_BANK, n_groups))
+            bank = transpose_slots(e_words, slots)
+            nc.scalar.copy(
+                out=words_view(e_grouped[:], n_groups)[:, first : first + len(slots)],
+                in_=bank_source(bank, len(slots)),
+            )
+        for i in range(n_groups):
+            nc.vector.quantize_mx(
+                out=e_codes[:, i, :].bitcast(FP8X4),
+                scales=e_scales[:, i, :],
+                in_=e_grouped[:, i * P * PACK : (i + 1) * P * PACK],
+            )
+
+        for n in range(n_rounds + 2):
+            if n + AHEAD < n_rounds:
+                load_round(n + AHEAD)
+            if n < n_rounds:
+                transpose_round(n)
+            if 1 <= n <= n_rounds:
+                multiply_round(n - 1)
+                subtract_round(n - 1)
+            if n < n_rounds:
+                quantise_round(n)
+            if n >= 2:
+                square_round(n - 2)
+
+        nc.vector.tensor_reduce(out=norm_sq[:], in_=sq_sums[:], axis=mybir.AxisListType.X, op=ALU.add)
+        nc.vector.tensor_scalar_max(out=floored[:], in0=norm_sq[:], scalar1=1.0)
+        nc.scalar.activation(out=norm_b[:], in_=floored[:], func=ACT.Sqrt, scale=float(P * P))
+        nc.vector.reciprocal(out=c_window[:, WINDOW - 1 : WINDOW], in_=norm_b[:])
+
+        sums = acc_pool.tile([P, CHUNK], F32, name="sums", tag="acc")
+        for m in range(n_col_tiles):
+            w, s = divmod(m, WINDOW)
+            n, j = divmod(m * P, round_cols)
+            nc.tensor.matmul(
+                out=sums[:, w * WINDOW : (w + 1) * WINDOW],
+                lhsT=r_tiles[n][:, j : j + P],
+                rhs=c_window[:, WINDOW - 1 - s : 2 * WINDOW - 1 - s],
+                start=(s == 0),
+                stop=(s == WINDOW - 1),
+            )
+
+        nc.vector.tensor_copy(out=out_cols[:, 0:n_col_tiles], in_=sums[:, 0:n_col_tiles])
+        flipped = acc_pool.tile([P, CHUNK], F32, name="flipped", tag="acc")
+        for h in range(2):
+            nc.tensor.transpose(flipped[:, h * P : (h + 1) * P], out_cols[:, h * P : (h + 1) * P], ident[:])
+        nc.vector.tensor_copy(out=out_rows[:], in_=flipped[:, 0 : 2 * P])
+        out_2d = out.rearrange("(m j) -> m j", j=P)
+        nc.sync.dma_start(out=out_2d[0:P, :], in_=out_rows[:, 0:P])
+        nc.scalar.dma_start(out=out_2d[P:n_col_tiles, :], in_=out_rows[0 : n_col_tiles - P, P : 2 * P])

@@ -21,7 +21,7 @@ SLOTS_PER_BANK = 2
 ROUND = 2
 G_ROUNDS = 2
 AHEAD = 3
-WINDOW = 32
+TILES_PER_BANK = 4
 
 FLOPS = 2 * 128 * 20480 * 512
 
@@ -65,7 +65,7 @@ def tile_gep_pb_kernel(tc, target_grad, embedding, bases0, bases1, bases2, out):
         norm_sq = keep.tile([P, 1], F32, name="norm_sq")
         floored = keep.tile([P, 1], F32, name="floored")
         norm_b = keep.tile([P, 1], F32, name="norm_b")
-        c_window = keep.tile([P, 2 * WINDOW - 1], F32, name="c_window")
+        c_over_b = keep.tile([P, 1], F32, name="c_over_b")
         out_cols = keep.tile([P, 2 * P], F32, name="out_cols")
         out_rows = keep.tile([P, 2 * P], F32, name="out_rows")
 
@@ -160,7 +160,6 @@ def tile_gep_pb_kernel(tc, target_grad, embedding, bases0, bases1, bases2, out):
             load_round(n)
         make_identity(nc, ident[:])
         nc.vector.memset(one[:], 1.0)
-        nc.vector.memset(c_window[:], 0.0)
         nc.vector.memset(out_cols[:], 0.0)
         nc.scalar.activation(out=warm[:], in_=one[:], func=ACT.Sqrt)
 
@@ -195,21 +194,22 @@ def tile_gep_pb_kernel(tc, target_grad, embedding, bases0, bases1, bases2, out):
         nc.vector.tensor_reduce(out=norm_sq[:], in_=sq_sums[:], axis=mybir.AxisListType.X, op=ALU.add)
         nc.vector.tensor_scalar_max(out=floored[:], in0=norm_sq[:], scalar1=1.0)
         nc.scalar.activation(out=norm_b[:], in_=floored[:], func=ACT.Sqrt, scale=float(P * P))
-        nc.vector.reciprocal(out=c_window[:, WINDOW - 1 : WINDOW], in_=norm_b[:])
+        nc.vector.reciprocal(out=c_over_b[:], in_=norm_b[:])
 
-        sums = acc_pool.tile([P, CHUNK], F32, name="sums", tag="acc")
-        for m in range(n_col_tiles):
-            w, s = divmod(m, WINDOW)
-            n, j = divmod(m * P, round_cols)
-            nc.tensor.matmul(
-                out=sums[:, w * WINDOW : (w + 1) * WINDOW],
-                lhsT=r_tiles[n][:, j : j + P],
-                rhs=c_window[:, WINDOW - 1 - s : 2 * WINDOW - 1 - s],
-                start=(s == 0),
-                stop=(s == WINDOW - 1),
+        for first in range(0, n_col_tiles, TILES_PER_BANK):
+            n, j = divmod(first * P, round_cols)
+            scaled = r_tiles[n][:, j : j + TILES_PER_BANK * P]
+            nc.scalar.activation(out=scaled, in_=scaled, func=ACT.Copy, scale=c_over_b[:])
+            turned = xt_pool.tile([P, TILES_PER_BANK, P], F32, name="turned", tag="xt")
+            for s in range(TILES_PER_BANK):
+                nc.tensor.transpose(turned[:, s, :], scaled[:, s * P : (s + 1) * P], ident[:])
+            nc.vector.tensor_reduce(
+                out=out_cols[:, first : first + TILES_PER_BANK],
+                in_=turned[:],
+                axis=mybir.AxisListType.X,
+                op=ALU.add,
             )
 
-        nc.vector.tensor_copy(out=out_cols[:, 0:n_col_tiles], in_=sums[:, 0:n_col_tiles])
         flipped = acc_pool.tile([P, CHUNK], F32, name="flipped", tag="acc")
         for h in range(2):
             nc.tensor.transpose(flipped[:, h * P : (h + 1) * P], out_cols[:, h * P : (h + 1) * P], ident[:])

@@ -22,6 +22,8 @@ ROUND = 2
 G_ROUNDS = 2
 AHEAD = 3
 TILES_PER_BANK = 4
+PERIOD = 5
+LEAD = 6
 
 FLOPS = 2 * 128 * 20480 * 512
 
@@ -196,19 +198,50 @@ def tile_gep_pb_kernel(tc, target_grad, embedding, bases0, bases1, bases2, out):
         nc.scalar.activation(out=norm_b[:], in_=floored[:], func=ACT.Sqrt, scale=float(P * P))
         nc.vector.reciprocal(out=c_over_b[:], in_=norm_b[:])
 
-        for first in range(0, n_col_tiles, TILES_PER_BANK):
-            n, j = divmod(first * P, round_cols)
-            scaled = r_tiles[n][:, j : j + TILES_PER_BANK * P]
-            nc.scalar.activation(out=scaled, in_=scaled, func=ACT.Copy, scale=c_over_b[:])
+        n_banks = n_col_tiles // TILES_PER_BANK
+
+        def bank_columns(q):
+            n, j = divmod(q * CHUNK, round_cols)
+            return r_tiles[n][:, j : j + CHUNK]
+
+        def scale_bank(q):
+            cols = bank_columns(q)
+            if (q // ROUND) % PERIOD in (0, 2):
+                nc.scalar.activation(out=cols, in_=cols, func=ACT.Copy, scale=c_over_b[:])
+            else:
+                nc.gpsimd.tensor_scalar(
+                    out=cols, in0=cols, scalar1=c_over_b[:], scalar2=0.0, op0=ALU.mult, op1=ALU.add
+                )
+
+        def sum_bank(q):
+            cols = bank_columns(q)
             turned = xt_pool.tile([P, TILES_PER_BANK, P], F32, name="turned", tag="xt")
             for s in range(TILES_PER_BANK):
-                nc.tensor.transpose(turned[:, s, :], scaled[:, s * P : (s + 1) * P], ident[:])
-            nc.vector.tensor_reduce(
-                out=out_cols[:, first : first + TILES_PER_BANK],
-                in_=turned[:],
-                axis=mybir.AxisListType.X,
-                op=ALU.add,
-            )
+                nc.tensor.transpose(turned[:, s, :], cols[:, s * P : (s + 1) * P], ident[:])
+            first = q * TILES_PER_BANK
+            if (q // ROUND) % PERIOD == PERIOD - 1:
+                copied = stage.tile([P, TILES_PER_BANK, P], BF16, name="copied")
+                for s in range(TILES_PER_BANK):
+                    nc.scalar.activation(
+                        out=copied[:, s, :],
+                        in_=turned[:, s, :],
+                        func=ACT.Copy,
+                        accum_out=out_cols[:, first + s : first + s + 1],
+                    )
+            else:
+                nc.vector.tensor_reduce(
+                    out=out_cols[:, first : first + TILES_PER_BANK],
+                    in_=turned[:],
+                    axis=mybir.AxisListType.X,
+                    op=ALU.add,
+                )
+
+        for q in range(LEAD):
+            scale_bank(q)
+        for q in range(n_banks):
+            if q + LEAD < n_banks:
+                scale_bank(q + LEAD)
+            sum_bank(q)
 
         flipped = acc_pool.tile([P, CHUNK], F32, name="flipped", tag="acc")
         for h in range(2):

@@ -10,6 +10,7 @@ U8 = mybir.dt.uint8
 FP8X4 = mybir.dt.float8_e4m3fn_x4
 ALU = mybir.AluOpType
 ACT = mybir.ActivationFunctionType
+X_AXIS = mybir.AxisListType.X
 
 P = 128
 K = 512
@@ -18,11 +19,12 @@ HALVES = 2
 SLOTS = 4
 CHUNK = P * SLOTS
 SLOTS_PER_BANK = 2
-ROUND = 2
-G_ROUNDS = 2
-AHEAD = 3
 TILES_PER_BANK = 4
-PERIOD = 5
+G_CHUNKS = 4
+AHEAD = 6
+XT_BANKS = 6
+ACC_BANKS = 2
+PERIOD = 10
 LEAD = 6
 
 FLOPS = 2 * 128 * 20480 * 512
@@ -39,16 +41,15 @@ def tile_gep_pb_kernel(tc, target_grad, embedding, bases0, bases1, bases2, out):
         for first in range(0, bases.shape[0], CHUNK):
             chunk_group.append(i)
             chunk_rows.append(bases[first : first + CHUNK, :])
-    n_rounds = len(chunk_rows) // ROUND
-    round_cols = ROUND * CHUNK
-    n_col_tiles = n_rounds * round_cols // P
+    n_chunks = len(chunk_rows)
+    n_col_tiles = n_chunks * TILES_PER_BANK
 
     with ExitStack() as stack:
         keep = stack.enter_context(tc.tile_pool(name="keep", bufs=1))
-        raw_pool = stack.enter_context(tc.tile_pool(name="raw_pool", bufs=(AHEAD + 1) * ROUND))
-        stage = stack.enter_context(tc.tile_pool(name="stage", bufs=2 * ROUND))
-        xt_pool = stack.enter_context(tc.psum_pool(name="xt_pool", bufs=6))
-        acc_pool = stack.enter_context(tc.psum_pool(name="acc_pool", bufs=ROUND))
+        raw_pool = stack.enter_context(tc.tile_pool(name="raw_pool", bufs=AHEAD + 2))
+        stage = stack.enter_context(tc.tile_pool(name="stage", bufs=4))
+        xt_pool = stack.enter_context(tc.psum_pool(name="xt_pool", bufs=XT_BANKS))
+        acc_pool = stack.enter_context(tc.psum_pool(name="acc_pool", bufs=ACC_BANKS))
         stack.enter_context(tc.manual_schedule())
 
         ident = keep.tile([P, P], F32, name="ident")
@@ -57,11 +58,10 @@ def tile_gep_pb_kernel(tc, target_grad, embedding, bases0, bases1, bases2, out):
         e_codes = keep.tile([P, n_groups, P], U32, name="e_codes", align_bytes=64)
         e_scales = keep.tile([P, n_groups, P], U8, name="e_scales", align_bytes=64)
         g_tiles = [
-            keep.tile([P, G_ROUNDS * round_cols], BF16, name="g%d" % q)
-            for q in range(n_rounds // G_ROUNDS)
+            keep.tile([P, G_CHUNKS * CHUNK], BF16, name="g%d" % q) for q in range(n_chunks // G_CHUNKS)
         ]
-        r_tiles = [keep.tile([P, round_cols], F32, name="r%d" % n) for n in range(n_rounds)]
-        sq_sums = keep.tile([P, n_rounds], F32, name="sq_sums")
+        residual = [keep.tile([P, CHUNK], F32, name="r%d" % c) for c in range(n_chunks)]
+        sq_sums = keep.tile([P, n_chunks], F32, name="sq_sums")
         one = keep.tile([P, 1], F32, name="one")
         warm = keep.tile([P, 1], F32, name="warm")
         norm_sq = keep.tile([P, 1], F32, name="norm_sq")
@@ -77,15 +77,12 @@ def tile_gep_pb_kernel(tc, target_grad, embedding, bases0, bases1, bases2, out):
         scales = {}
         acc = {}
 
-        def load_round(n):
-            for c in range(n * ROUND, (n + 1) * ROUND):
-                raw[c] = raw_pool.tile([P, SLOTS, K], BF16, name="raw")
-                nc.sync.dma_start(
-                    out=raw[c][:], in_=chunk_rows[c].rearrange("(p t) k -> p t k", t=SLOTS)
-                )
-            if n % G_ROUNDS == 0:
-                q = n // G_ROUNDS
-                width = G_ROUNDS * round_cols
+        def load(c):
+            raw[c] = raw_pool.tile([P, SLOTS, K], BF16, name="raw")
+            nc.sync.dma_start(out=raw[c][:], in_=chunk_rows[c].rearrange("(p t) k -> p t k", t=SLOTS))
+            if c % G_CHUNKS == 0:
+                q = c // G_CHUNKS
+                width = G_CHUNKS * CHUNK
                 nc.sync.dma_start(out=g_tiles[q][:], in_=target_grad[:, q * width : (q + 1) * width])
 
         def transpose_slots(words, slots):
@@ -101,65 +98,56 @@ def tile_gep_pb_kernel(tc, target_grad, embedding, bases0, bases1, bases2, out):
         def bank_source(bank, slots):
             return bank[:, 0:slots].rearrange("q t u p -> q t p u")
 
-        def transpose_round(n):
-            banks = []
-            for c in range(n * ROUND, (n + 1) * ROUND):
-                words = raw[c][:].bitcast(F32)
-                for first in range(0, SLOTS, SLOTS_PER_BANK):
-                    banks.append((c, first, transpose_slots(words, range(first, first + SLOTS_PER_BANK))))
-            for c in range(n * ROUND, (n + 1) * ROUND):
-                grouped[c] = stage.tile([P, CHUNK * PACK], BF16, name="grouped", align_bytes=64)
-            for b, (c, first, bank) in enumerate(banks):
-                dst = words_view(grouped[c][:], SLOTS)[:, first : first + SLOTS_PER_BANK]
-                if b == len(banks) - 1:
+        def transpose(c):
+            words = raw[c][:].bitcast(F32)
+            banks = [
+                transpose_slots(words, range(first, first + SLOTS_PER_BANK))
+                for first in range(0, SLOTS, SLOTS_PER_BANK)
+            ]
+            grouped[c] = stage.tile([P, CHUNK * PACK], BF16, name="grouped", align_bytes=64)
+            for h, bank in enumerate(banks):
+                dst = words_view(grouped[c][:], SLOTS)[:, h * SLOTS_PER_BANK : (h + 1) * SLOTS_PER_BANK]
+                if c % 2 == 1 and h == 1:
                     nc.vector.tensor_copy(out=dst, in_=bank_source(bank, SLOTS_PER_BANK))
                 else:
                     nc.scalar.copy(out=dst, in_=bank_source(bank, SLOTS_PER_BANK))
 
-        def quantise_round(n):
-            for c in range(n * ROUND, (n + 1) * ROUND):
-                codes[c] = stage.tile([P, CHUNK], U32, name="codes", align_bytes=64)
-                scales[c] = stage.tile([P, CHUNK], U8, name="scales", align_bytes=64)
-                nc.vector.quantize_mx(
-                    out=codes[c][:].bitcast(FP8X4), scales=scales[c][:], in_=grouped[c][:]
-                )
+        def quantise(c):
+            codes[c] = stage.tile([P, CHUNK], U32, name="codes", align_bytes=64)
+            scales[c] = stage.tile([P, CHUNK], U8, name="scales", align_bytes=64)
+            nc.vector.quantize_mx(out=codes[c][:].bitcast(FP8X4), scales=scales[c][:], in_=grouped[c][:])
 
-        def multiply_round(n):
-            for c in range(n * ROUND, (n + 1) * ROUND):
-                i = chunk_group[c]
-                acc[c] = acc_pool.tile([P, CHUNK], F32, name="acc")
-                nc.tensor.matmul_mx(
-                    out=acc[c][:],
-                    lhsT=e_codes[:, i, :].bitcast(FP8X4),
-                    lhsT_scale=e_scales[:, i, :],
-                    rhs=codes[c][:].bitcast(FP8X4),
-                    rhs_scale=scales[c][:],
-                    start=True,
-                    stop=True,
-                )
+        def multiply(c):
+            i = chunk_group[c]
+            acc[c] = acc_pool.tile([P, CHUNK], F32, name="acc")
+            nc.tensor.matmul_mx(
+                out=acc[c][:],
+                lhsT=e_codes[:, i, :].bitcast(FP8X4),
+                lhsT_scale=e_scales[:, i, :],
+                rhs=codes[c][:].bitcast(FP8X4),
+                rhs_scale=scales[c][:],
+                start=True,
+                stop=True,
+            )
 
-        def subtract_round(n):
-            for h in range(ROUND):
-                c = n * ROUND + h
-                g_first = (n % G_ROUNDS) * round_cols + h * CHUNK
-                nc.vector.tensor_tensor(
-                    out=r_tiles[n][:, h * CHUNK : (h + 1) * CHUNK].rearrange("b (p t) -> b p t", t=SLOTS),
-                    in0=g_tiles[n // G_ROUNDS][:, g_first : g_first + CHUNK].rearrange(
-                        "b (p t) -> b p t", t=SLOTS
-                    ),
-                    in1=acc[c][:].rearrange("b (t p) -> b p t", t=SLOTS),
-                    op=ALU.subtract,
-                )
+        def subtract(c):
+            g_first = (c % G_CHUNKS) * CHUNK
+            nc.vector.tensor_tensor(
+                out=residual[c][:].rearrange("b (p t) -> b p t", t=SLOTS),
+                in0=g_tiles[c // G_CHUNKS][:, g_first : g_first + CHUNK].rearrange("b (p t) -> b p t", t=SLOTS),
+                in1=acc[c][:].rearrange("b (t p) -> b p t", t=SLOTS),
+                op=ALU.subtract,
+            )
 
-        def square_round(n):
-            squares = stage.tile([P, round_cols], BF16, name="squares")
+        def square(c):
+            squares = stage.tile([P, CHUNK], BF16, name="squares")
             nc.scalar.activation(
-                out=squares[:], in_=r_tiles[n][:], func=ACT.Square, accum_out=sq_sums[:, n : n + 1]
+                out=squares[:], in_=residual[c][:], func=ACT.Square, accum_out=sq_sums[:, c : c + 1]
             )
 
         nc.sync.dma_start(out=e_sb[:], in_=embedding.rearrange("b (i k) -> b i k", k=K))
-        for n in range(AHEAD):
-            load_round(n)
+        for c in range(AHEAD):
+            load(c)
         make_identity(nc, ident[:])
         nc.vector.memset(one[:], 1.0)
         nc.vector.memset(out_cols[:], 0.0)
@@ -180,46 +168,44 @@ def tile_gep_pb_kernel(tc, target_grad, embedding, bases0, bases1, bases2, out):
                 in_=e_grouped[:, i * P * PACK : (i + 1) * P * PACK],
             )
 
-        for n in range(n_rounds + 2):
-            if n + AHEAD < n_rounds:
-                load_round(n + AHEAD)
-            if n < n_rounds:
-                transpose_round(n)
-            if 1 <= n <= n_rounds:
-                multiply_round(n - 1)
-                subtract_round(n - 1)
-            if n < n_rounds:
-                quantise_round(n)
-            if n >= 2:
-                square_round(n - 2)
+        for c in range(n_chunks + 3):
+            if c + AHEAD < n_chunks:
+                load(c + AHEAD)
+            if c < n_chunks:
+                transpose(c)
+            if 0 <= c - 1 < n_chunks:
+                multiply(c - 1)
+            if 0 <= c - 2 < n_chunks:
+                subtract(c - 2)
+            if c < n_chunks:
+                quantise(c)
+            if 0 <= c - 3:
+                square(c - 3)
 
-        nc.vector.tensor_reduce(out=norm_sq[:], in_=sq_sums[:], axis=mybir.AxisListType.X, op=ALU.add)
+        nc.vector.tensor_reduce(out=norm_sq[:], in_=sq_sums[:], axis=X_AXIS, op=ALU.add)
         nc.vector.tensor_scalar_max(out=floored[:], in0=norm_sq[:], scalar1=1.0)
         nc.scalar.activation(out=norm_b[:], in_=floored[:], func=ACT.Sqrt, scale=float(P * P))
         nc.vector.reciprocal(out=c_over_b[:], in_=norm_b[:])
 
-        n_banks = n_col_tiles // TILES_PER_BANK
-
-        def bank_columns(q):
-            n, j = divmod(q * CHUNK, round_cols)
-            return r_tiles[n][:, j : j + CHUNK]
-
-        def scale_bank(q):
-            cols = bank_columns(q)
-            if (q // ROUND) % PERIOD in (0, 2):
-                nc.scalar.activation(out=cols, in_=cols, func=ACT.Copy, scale=c_over_b[:])
+        def scale(c):
+            if c % PERIOD in (0, 1, 4, 5):
+                nc.scalar.activation(out=residual[c][:], in_=residual[c][:], func=ACT.Copy, scale=c_over_b[:])
             else:
                 nc.gpsimd.tensor_scalar(
-                    out=cols, in0=cols, scalar1=c_over_b[:], scalar2=0.0, op0=ALU.mult, op1=ALU.add
+                    out=residual[c][:],
+                    in0=residual[c][:],
+                    scalar1=c_over_b[:],
+                    scalar2=0.0,
+                    op0=ALU.mult,
+                    op1=ALU.add,
                 )
 
-        def sum_bank(q):
-            cols = bank_columns(q)
+        def sum_over_batch(c):
             turned = xt_pool.tile([P, TILES_PER_BANK, P], F32, name="turned", tag="xt")
             for s in range(TILES_PER_BANK):
-                nc.tensor.transpose(turned[:, s, :], cols[:, s * P : (s + 1) * P], ident[:])
-            first = q * TILES_PER_BANK
-            if (q // ROUND) % PERIOD == PERIOD - 1:
+                nc.tensor.transpose(turned[:, s, :], residual[c][:, s * P : (s + 1) * P], ident[:])
+            first = c * TILES_PER_BANK
+            if c % PERIOD >= PERIOD - 2:
                 copied = stage.tile([P, TILES_PER_BANK, P], BF16, name="copied")
                 for s in range(TILES_PER_BANK):
                     nc.scalar.activation(
@@ -230,18 +216,15 @@ def tile_gep_pb_kernel(tc, target_grad, embedding, bases0, bases1, bases2, out):
                     )
             else:
                 nc.vector.tensor_reduce(
-                    out=out_cols[:, first : first + TILES_PER_BANK],
-                    in_=turned[:],
-                    axis=mybir.AxisListType.X,
-                    op=ALU.add,
+                    out=out_cols[:, first : first + TILES_PER_BANK], in_=turned[:], axis=X_AXIS, op=ALU.add
                 )
 
-        for q in range(LEAD):
-            scale_bank(q)
-        for q in range(n_banks):
-            if q + LEAD < n_banks:
-                scale_bank(q + LEAD)
-            sum_bank(q)
+        for c in range(LEAD):
+            scale(c)
+        for c in range(n_chunks):
+            if c + LEAD < n_chunks:
+                scale(c + LEAD)
+            sum_over_batch(c)
 
         flipped = acc_pool.tile([P, CHUNK], F32, name="flipped", tag="acc")
         for h in range(2):

@@ -10,7 +10,6 @@ U8 = mybir.dt.uint8
 FP8X4 = mybir.dt.float8_e4m3fn_x4
 ALU = mybir.AluOpType
 ACT = mybir.ActivationFunctionType
-X_AXIS = mybir.AxisListType.X
 
 P = 128
 K = 512
@@ -19,13 +18,12 @@ HALVES = 2
 SLOTS = 4
 CHUNK = P * SLOTS
 SLOTS_PER_BANK = 2
+ROUND = 2
+G_ROUNDS = 2
+AHEAD = 3
 TILES_PER_BANK = 4
-G_CHUNKS = 4
-AHEAD = 6
-XT_BANKS = 6
-ACC_BANKS = 2
-PERIOD = 10
-LEAD = 6
+PERIOD = 5
+LEAD = 3
 
 FLOPS = 2 * 128 * 20480 * 512
 
@@ -41,15 +39,16 @@ def tile_gep_pb_kernel(tc, target_grad, embedding, bases0, bases1, bases2, out):
         for first in range(0, bases.shape[0], CHUNK):
             chunk_group.append(i)
             chunk_rows.append(bases[first : first + CHUNK, :])
-    n_chunks = len(chunk_rows)
-    n_col_tiles = n_chunks * TILES_PER_BANK
+    n_rounds = len(chunk_rows) // ROUND
+    round_cols = ROUND * CHUNK
+    n_col_tiles = n_rounds * round_cols // P
 
     with ExitStack() as stack:
         keep = stack.enter_context(tc.tile_pool(name="keep", bufs=1))
-        raw_pool = stack.enter_context(tc.tile_pool(name="raw_pool", bufs=AHEAD + 2))
-        stage = stack.enter_context(tc.tile_pool(name="stage", bufs=4))
-        xt_pool = stack.enter_context(tc.psum_pool(name="xt_pool", bufs=XT_BANKS))
-        acc_pool = stack.enter_context(tc.psum_pool(name="acc_pool", bufs=ACC_BANKS))
+        raw_pool = stack.enter_context(tc.tile_pool(name="raw_pool", bufs=(AHEAD + 1) * ROUND))
+        stage = stack.enter_context(tc.tile_pool(name="stage", bufs=2 * ROUND))
+        xt_pool = stack.enter_context(tc.psum_pool(name="xt_pool", bufs=6))
+        acc_pool = stack.enter_context(tc.psum_pool(name="acc_pool", bufs=ROUND))
         stack.enter_context(tc.manual_schedule())
 
         ident = keep.tile([P, P], F32, name="ident")
@@ -58,10 +57,11 @@ def tile_gep_pb_kernel(tc, target_grad, embedding, bases0, bases1, bases2, out):
         e_codes = keep.tile([P, n_groups, P], U32, name="e_codes", align_bytes=64)
         e_scales = keep.tile([P, n_groups, P], U8, name="e_scales", align_bytes=64)
         g_tiles = [
-            keep.tile([P, G_CHUNKS * CHUNK], BF16, name="g%d" % q) for q in range(n_chunks // G_CHUNKS)
+            keep.tile([P, G_ROUNDS * round_cols], BF16, name="g%d" % q)
+            for q in range(n_rounds // G_ROUNDS)
         ]
-        residual = [keep.tile([P, CHUNK], F32, name="r%d" % c) for c in range(n_chunks)]
-        sq_sums = keep.tile([P, n_chunks], F32, name="sq_sums")
+        r_tiles = [keep.tile([P, round_cols], F32, name="r%d" % n) for n in range(n_rounds)]
+        sq_sums = keep.tile([P, n_rounds], F32, name="sq_sums")
         one = keep.tile([P, 1], F32, name="one")
         warm = keep.tile([P, 1], F32, name="warm")
         norm_sq = keep.tile([P, 1], F32, name="norm_sq")
@@ -77,12 +77,17 @@ def tile_gep_pb_kernel(tc, target_grad, embedding, bases0, bases1, bases2, out):
         scales = {}
         acc = {}
 
-        def load(c):
-            raw[c] = raw_pool.tile([P, SLOTS, K], BF16, name="raw")
-            nc.sync.dma_start(out=raw[c][:], in_=chunk_rows[c].rearrange("(p t) k -> p t k", t=SLOTS))
-            if c % G_CHUNKS == 0:
-                q = c // G_CHUNKS
-                width = G_CHUNKS * CHUNK
+        def load_round(n):
+            for c in range(n * ROUND, (n + 1) * ROUND):
+                raw[c] = raw_pool.tile([P, SLOTS, K], BF16, name="raw")
+                nc.sync.dma_start(
+                    out=raw[c][:], in_=chunk_rows[c].rearrange("(p t) k -> p t k", t=SLOTS)
+                )
+
+        def load_grad(n):
+            if n % G_ROUNDS == 0:
+                q = n // G_ROUNDS
+                width = G_ROUNDS * round_cols
                 nc.sync.dma_start(out=g_tiles[q][:], in_=target_grad[:, q * width : (q + 1) * width])
 
         def transpose_slots(words, slots):
@@ -98,61 +103,75 @@ def tile_gep_pb_kernel(tc, target_grad, embedding, bases0, bases1, bases2, out):
         def bank_source(bank, slots):
             return bank[:, 0:slots].rearrange("q t u p -> q t p u")
 
-        def transpose(c):
-            words = raw[c][:].bitcast(F32)
-            banks = [
-                transpose_slots(words, range(first, first + SLOTS_PER_BANK))
-                for first in range(0, SLOTS, SLOTS_PER_BANK)
-            ]
-            grouped[c] = stage.tile([P, CHUNK * PACK], BF16, name="grouped", align_bytes=64)
-            for h, bank in enumerate(banks):
-                dst = words_view(grouped[c][:], SLOTS)[:, h * SLOTS_PER_BANK : (h + 1) * SLOTS_PER_BANK]
-                if c % 2 == 1 and h == 1:
+        def transpose_round(n):
+            banks = []
+            for c in range(n * ROUND, (n + 1) * ROUND):
+                words = raw[c][:].bitcast(F32)
+                for first in range(0, SLOTS, SLOTS_PER_BANK):
+                    banks.append((c, first, transpose_slots(words, range(first, first + SLOTS_PER_BANK))))
+            for c in range(n * ROUND, (n + 1) * ROUND):
+                grouped[c] = stage.tile([P, CHUNK * PACK], BF16, name="grouped", align_bytes=64)
+            for b, (c, first, bank) in enumerate(banks):
+                dst = words_view(grouped[c][:], SLOTS)[:, first : first + SLOTS_PER_BANK]
+                if b == len(banks) - 1:
                     nc.vector.tensor_copy(out=dst, in_=bank_source(bank, SLOTS_PER_BANK))
                 else:
                     nc.scalar.copy(out=dst, in_=bank_source(bank, SLOTS_PER_BANK))
 
-        def quantise(c):
-            codes[c] = stage.tile([P, CHUNK], U32, name="codes", align_bytes=64)
-            scales[c] = stage.tile([P, CHUNK], U8, name="scales", align_bytes=64)
-            nc.vector.quantize_mx(out=codes[c][:].bitcast(FP8X4), scales=scales[c][:], in_=grouped[c][:])
+        def quantise_round(n):
+            for c in range(n * ROUND, (n + 1) * ROUND):
+                codes[c] = stage.tile([P, CHUNK], U32, name="codes", align_bytes=64)
+                scales[c] = stage.tile([P, CHUNK], U8, name="scales", align_bytes=64)
+                nc.vector.quantize_mx(
+                    out=codes[c][:].bitcast(FP8X4), scales=scales[c][:], in_=grouped[c][:]
+                )
 
-        def multiply(c):
-            i = chunk_group[c]
-            acc[c] = acc_pool.tile([P, CHUNK], F32, name="acc")
-            nc.tensor.matmul_mx(
-                out=acc[c][:],
-                lhsT=e_codes[:, i, :].bitcast(FP8X4),
-                lhsT_scale=e_scales[:, i, :],
-                rhs=codes[c][:].bitcast(FP8X4),
-                rhs_scale=scales[c][:],
-                start=True,
-                stop=True,
-            )
+        def multiply_round(n):
+            for c in range(n * ROUND, (n + 1) * ROUND):
+                i = chunk_group[c]
+                acc[c] = acc_pool.tile([P, CHUNK], F32, name="acc")
+                nc.tensor.matmul_mx(
+                    out=acc[c][:],
+                    lhsT=e_codes[:, i, :].bitcast(FP8X4),
+                    lhsT_scale=e_scales[:, i, :],
+                    rhs=codes[c][:].bitcast(FP8X4),
+                    rhs_scale=scales[c][:],
+                    start=True,
+                    stop=True,
+                )
 
-        def subtract(c):
-            g_first = (c % G_CHUNKS) * CHUNK
-            nc.vector.tensor_tensor(
-                out=residual[c][:].rearrange("b (p t) -> b p t", t=SLOTS),
-                in0=g_tiles[c // G_CHUNKS][:, g_first : g_first + CHUNK].rearrange("b (p t) -> b p t", t=SLOTS),
-                in1=acc[c][:].rearrange("b (t p) -> b p t", t=SLOTS),
-                op=ALU.subtract,
-            )
+        def subtract_round(n):
+            for h in range(ROUND):
+                c = n * ROUND + h
+                g_first = (n % G_ROUNDS) * round_cols + h * CHUNK
+                nc.vector.tensor_tensor(
+                    out=r_tiles[n][:, h * CHUNK : (h + 1) * CHUNK].rearrange("b (p t) -> b p t", t=SLOTS),
+                    in0=g_tiles[n // G_ROUNDS][:, g_first : g_first + CHUNK].rearrange(
+                        "b (p t) -> b p t", t=SLOTS
+                    ),
+                    in1=acc[c][:].rearrange("b (t p) -> b p t", t=SLOTS),
+                    op=ALU.subtract,
+                )
 
-        def square(c):
-            squares = stage.tile([P, CHUNK], BF16, name="squares")
+        def square_round(n):
+            squares = stage.tile([P, round_cols], BF16, name="squares")
             nc.scalar.activation(
-                out=squares[:], in_=residual[c][:], func=ACT.Square, accum_out=sq_sums[:, c : c + 1]
+                out=squares[:], in_=r_tiles[n][:], func=ACT.Square, accum_out=sq_sums[:, n : n + 1]
             )
 
+        load_round(0)
         nc.sync.dma_start(out=e_sb[:], in_=embedding.rearrange("b (i k) -> b i k", k=K))
-        for c in range(AHEAD):
-            load(c)
+        load_grad(0)
+        for n in range(1, AHEAD):
+            load_round(n)
+            load_grad(n)
         make_identity(nc, ident[:])
         nc.vector.memset(one[:], 1.0)
         nc.vector.memset(out_cols[:], 0.0)
         nc.scalar.activation(out=warm[:], in_=one[:], func=ACT.Sqrt)
 
+        transpose_round(0)
+        quantise_round(0)
         e_words = e_sb[:].bitcast(F32)
         for first in range(0, n_groups, SLOTS_PER_BANK):
             slots = range(first, min(first + SLOTS_PER_BANK, n_groups))
@@ -168,63 +187,70 @@ def tile_gep_pb_kernel(tc, target_grad, embedding, bases0, bases1, bases2, out):
                 in_=e_grouped[:, i * P * PACK : (i + 1) * P * PACK],
             )
 
-        for c in range(n_chunks + 3):
-            if c + AHEAD < n_chunks:
-                load(c + AHEAD)
-            if c < n_chunks:
-                transpose(c)
-            if 0 <= c - 1 < n_chunks:
-                multiply(c - 1)
-            if 0 <= c - 2 < n_chunks:
-                subtract(c - 2)
-            if c < n_chunks:
-                quantise(c)
-            if 0 <= c - 3:
-                square(c - 3)
+        for n in range(1, n_rounds + 2):
+            if n - 1 + AHEAD < n_rounds:
+                load_round(n - 1 + AHEAD)
+                load_grad(n - 1 + AHEAD)
+            if n < n_rounds:
+                transpose_round(n)
+            if n <= n_rounds:
+                multiply_round(n - 1)
+                subtract_round(n - 1)
+            if n < n_rounds:
+                quantise_round(n)
+            if n >= 2:
+                square_round(n - 2)
 
-        nc.vector.tensor_reduce(out=norm_sq[:], in_=sq_sums[:], axis=X_AXIS, op=ALU.add)
+        nc.vector.tensor_reduce(out=norm_sq[:], in_=sq_sums[:], axis=mybir.AxisListType.X, op=ALU.add)
         nc.vector.tensor_scalar_max(out=floored[:], in0=norm_sq[:], scalar1=1.0)
         nc.scalar.activation(out=norm_b[:], in_=floored[:], func=ACT.Sqrt, scale=float(P * P))
         nc.vector.reciprocal(out=c_over_b[:], in_=norm_b[:])
 
-        def scale(c):
-            if c % PERIOD in (0, 1, 4, 5):
-                nc.scalar.activation(out=residual[c][:], in_=residual[c][:], func=ACT.Copy, scale=c_over_b[:])
+        def scale_round(n):
+            if n % PERIOD in (0, 3):
+                for h in range(ROUND):
+                    cols = r_tiles[n][:, h * CHUNK : (h + 1) * CHUNK]
+                    nc.scalar.activation(out=cols, in_=cols, func=ACT.Copy, scale=c_over_b[:])
             else:
                 nc.gpsimd.tensor_scalar(
-                    out=residual[c][:],
-                    in0=residual[c][:],
+                    out=r_tiles[n][:],
+                    in0=r_tiles[n][:],
                     scalar1=c_over_b[:],
                     scalar2=0.0,
                     op0=ALU.mult,
                     op1=ALU.add,
                 )
 
-        def sum_over_batch(c):
-            turned = xt_pool.tile([P, TILES_PER_BANK, P], F32, name="turned", tag="xt")
-            for s in range(TILES_PER_BANK):
-                nc.tensor.transpose(turned[:, s, :], residual[c][:, s * P : (s + 1) * P], ident[:])
-            first = c * TILES_PER_BANK
-            if c % PERIOD >= PERIOD - 2:
-                copied = stage.tile([P, TILES_PER_BANK, P], BF16, name="copied")
+        def sum_round(n):
+            for h in range(ROUND):
+                turned = xt_pool.tile([P, TILES_PER_BANK, P], F32, name="turned", tag="xt")
                 for s in range(TILES_PER_BANK):
-                    nc.scalar.activation(
-                        out=copied[:, s, :],
-                        in_=turned[:, s, :],
-                        func=ACT.Copy,
-                        accum_out=out_cols[:, first + s : first + s + 1],
+                    j = (h * TILES_PER_BANK + s) * P
+                    nc.tensor.transpose(turned[:, s, :], r_tiles[n][:, j : j + P], ident[:])
+                first = (n * ROUND + h) * TILES_PER_BANK
+                if n % PERIOD == 2:
+                    copied = stage.tile([P, TILES_PER_BANK, P], BF16, name="copied")
+                    for s in range(TILES_PER_BANK):
+                        nc.scalar.activation(
+                            out=copied[:, s, :],
+                            in_=turned[:, s, :],
+                            func=ACT.Copy,
+                            accum_out=out_cols[:, first + s : first + s + 1],
+                        )
+                else:
+                    nc.vector.tensor_reduce(
+                        out=out_cols[:, first : first + TILES_PER_BANK],
+                        in_=turned[:],
+                        axis=mybir.AxisListType.X,
+                        op=ALU.add,
                     )
-            else:
-                nc.vector.tensor_reduce(
-                    out=out_cols[:, first : first + TILES_PER_BANK], in_=turned[:], axis=X_AXIS, op=ALU.add
-                )
 
-        for c in range(LEAD):
-            scale(c)
-        for c in range(n_chunks):
-            if c + LEAD < n_chunks:
-                scale(c + LEAD)
-            sum_over_batch(c)
+        for n in range(LEAD):
+            scale_round(n)
+        for n in range(n_rounds):
+            if n + LEAD < n_rounds:
+                scale_round(n + LEAD)
+            sum_round(n)
 
         flipped = acc_pool.tile([P, CHUNK], F32, name="flipped", tag="acc")
         for h in range(2):

from contextlib import ExitStack

import concourse.mybir as mybir
from concourse.masks import make_identity

F32 = mybir.dt.float32
BF16 = mybir.dt.bfloat16
U32 = mybir.dt.uint32
U8 = mybir.dt.uint8
FP8X4 = mybir.dt.float8_e4m3fn_x4
ALU = mybir.AluOpType
ACT = mybir.ActivationFunctionType

P = 128
K = 512
PACK = 4
HALVES = 2
SLOTS = 4
CHUNK = P * SLOTS
SLOTS_PER_BANK = 2
ROUND = 2
G_ROUNDS = 2
AHEAD = 3
TILES_PER_BANK = 4
PERIOD = 5
LEAD = 3

FLOPS = 2 * 128 * 20480 * 512


def tile_gep_pb_kernel(tc, target_grad, embedding, bases0, bases1, bases2, out):
    nc = tc.nc
    groups = (bases0, bases1, bases2)
    n_groups = len(groups)

    chunk_group = []
    chunk_rows = []
    for i, bases in enumerate(groups):
        for first in range(0, bases.shape[0], CHUNK):
            chunk_group.append(i)
            chunk_rows.append(bases[first : first + CHUNK, :])
    n_rounds = len(chunk_rows) // ROUND
    round_cols = ROUND * CHUNK
    n_col_tiles = n_rounds * round_cols // P

    with ExitStack() as stack:
        keep = stack.enter_context(tc.tile_pool(name="keep", bufs=1))
        raw_pool = stack.enter_context(tc.tile_pool(name="raw_pool", bufs=(AHEAD + 1) * ROUND))
        stage = stack.enter_context(tc.tile_pool(name="stage", bufs=2 * ROUND))
        xt_pool = stack.enter_context(tc.psum_pool(name="xt_pool", bufs=6))
        acc_pool = stack.enter_context(tc.psum_pool(name="acc_pool", bufs=ROUND))
        stack.enter_context(tc.manual_schedule())

        ident = keep.tile([P, P], F32, name="ident")
        e_sb = keep.tile([P, n_groups, K], BF16, name="e_sb")
        e_grouped = keep.tile([P, n_groups * P * PACK], BF16, name="e_grouped", align_bytes=64)
        e_codes = keep.tile([P, n_groups, P], U32, name="e_codes", align_bytes=64)
        e_scales = keep.tile([P, n_groups, P], U8, name="e_scales", align_bytes=64)
        g_tiles = [
            keep.tile([P, G_ROUNDS * round_cols], BF16, name="g%d" % q)
            for q in range(n_rounds // G_ROUNDS)
        ]
        r_tiles = [keep.tile([P, round_cols], F32, name="r%d" % n) for n in range(n_rounds)]
        sq_sums = keep.tile([P, n_rounds], F32, name="sq_sums")
        one = keep.tile([P, 1], F32, name="one")
        warm = keep.tile([P, 1], F32, name="warm")
        norm_sq = keep.tile([P, 1], F32, name="norm_sq")
        floored = keep.tile([P, 1], F32, name="floored")
        norm_b = keep.tile([P, 1], F32, name="norm_b")
        c_over_b = keep.tile([P, 1], F32, name="c_over_b")
        out_cols = keep.tile([P, 2 * P], F32, name="out_cols")
        out_rows = keep.tile([P, 2 * P], F32, name="out_rows")

        raw = {}
        grouped = {}
        codes = {}
        scales = {}
        acc = {}

        def load_round(n):
            for c in range(n * ROUND, (n + 1) * ROUND):
                raw[c] = raw_pool.tile([P, SLOTS, K], BF16, name="raw")
                nc.sync.dma_start(
                    out=raw[c][:], in_=chunk_rows[c].rearrange("(p t) k -> p t k", t=SLOTS)
                )

        def load_grad(n):
            if n % G_ROUNDS == 0:
                q = n // G_ROUNDS
                width = G_ROUNDS * round_cols
                nc.sync.dma_start(out=g_tiles[q][:], in_=target_grad[:, q * width : (q + 1) * width])

        def transpose_slots(words, slots):
            bank = xt_pool.tile([P, SLOTS_PER_BANK, HALVES, P], F32, name="xt")
            for s, t in enumerate(slots):
                for u in range(HALVES):
                    nc.tensor.transpose(bank[:, s, u, :], words[:, t, u * P : (u + 1) * P], ident[:])
            return bank

        def words_view(tile_ap, slots):
            return tile_ap.bitcast(F32).rearrange("q (t p u) -> q t p u", t=slots, u=HALVES)

        def bank_source(bank, slots):
            return bank[:, 0:slots].rearrange("q t u p -> q t p u")

        def transpose_round(n):
            banks = []
            for c in range(n * ROUND, (n + 1) * ROUND):
                words = raw[c][:].bitcast(F32)
                for first in range(0, SLOTS, SLOTS_PER_BANK):
                    banks.append((c, first, transpose_slots(words, range(first, first + SLOTS_PER_BANK))))
            for c in range(n * ROUND, (n + 1) * ROUND):
                grouped[c] = stage.tile([P, CHUNK * PACK], BF16, name="grouped", align_bytes=64)
            for b, (c, first, bank) in enumerate(banks):
                dst = words_view(grouped[c][:], SLOTS)[:, first : first + SLOTS_PER_BANK]
                if b == len(banks) - 1:
                    nc.vector.tensor_copy(out=dst, in_=bank_source(bank, SLOTS_PER_BANK))
                else:
                    nc.scalar.copy(out=dst, in_=bank_source(bank, SLOTS_PER_BANK))

        def quantise_round(n):
            for c in range(n * ROUND, (n + 1) * ROUND):
                codes[c] = stage.tile([P, CHUNK], U32, name="codes", align_bytes=64)
                scales[c] = stage.tile([P, CHUNK], U8, name="scales", align_bytes=64)
                nc.vector.quantize_mx(
                    out=codes[c][:].bitcast(FP8X4), scales=scales[c][:], in_=grouped[c][:]
                )

        def multiply_round(n):
            for c in range(n * ROUND, (n + 1) * ROUND):
                i = chunk_group[c]
                acc[c] = acc_pool.tile([P, CHUNK], F32, name="acc")
                nc.tensor.matmul_mx(
                    out=acc[c][:],
                    lhsT=e_codes[:, i, :].bitcast(FP8X4),
                    lhsT_scale=e_scales[:, i, :],
                    rhs=codes[c][:].bitcast(FP8X4),
                    rhs_scale=scales[c][:],
                    start=True,
                    stop=True,
                )

        def subtract_round(n):
            for h in range(ROUND):
                c = n * ROUND + h
                g_first = (n % G_ROUNDS) * round_cols + h * CHUNK
                nc.vector.tensor_tensor(
                    out=r_tiles[n][:, h * CHUNK : (h + 1) * CHUNK].rearrange("b (p t) -> b p t", t=SLOTS),
                    in0=g_tiles[n // G_ROUNDS][:, g_first : g_first + CHUNK].rearrange(
                        "b (p t) -> b p t", t=SLOTS
                    ),
                    in1=acc[c][:].rearrange("b (t p) -> b p t", t=SLOTS),
                    op=ALU.subtract,
                )

        def square_round(n):
            squares = stage.tile([P, round_cols], BF16, name="squares")
            nc.scalar.activation(
                out=squares[:], in_=r_tiles[n][:], func=ACT.Square, accum_out=sq_sums[:, n : n + 1]
            )

        load_round(0)
        nc.sync.dma_start(out=e_sb[:], in_=embedding.rearrange("b (i k) -> b i k", k=K))
        load_grad(0)
        for n in range(1, AHEAD):
            load_round(n)
            load_grad(n)
        make_identity(nc, ident[:])
        nc.vector.memset(one[:], 1.0)
        nc.vector.memset(out_cols[:], 0.0)
        nc.scalar.activation(out=warm[:], in_=one[:], func=ACT.Sqrt)

        transpose_round(0)
        quantise_round(0)
        e_words = e_sb[:].bitcast(F32)
        for first in range(0, n_groups, SLOTS_PER_BANK):
            slots = range(first, min(first + SLOTS_PER_BANK, n_groups))
            bank = transpose_slots(e_words, slots)
            nc.scalar.copy(
                out=words_view(e_grouped[:], n_groups)[:, first : first + len(slots)],
                in_=bank_source(bank, len(slots)),
            )
        for i in range(n_groups):
            nc.vector.quantize_mx(
                out=e_codes[:, i, :].bitcast(FP8X4),
                scales=e_scales[:, i, :],
                in_=e_grouped[:, i * P * PACK : (i + 1) * P * PACK],
            )

        for n in range(1, n_rounds + 2):
            if n - 1 + AHEAD < n_rounds:
                load_round(n - 1 + AHEAD)
                load_grad(n - 1 + AHEAD)
            if n < n_rounds:
                transpose_round(n)
            if n <= n_rounds:
                multiply_round(n - 1)
                subtract_round(n - 1)
            if n < n_rounds:
                quantise_round(n)
            if n >= 2:
                square_round(n - 2)

        nc.vector.tensor_reduce(out=norm_sq[:], in_=sq_sums[:], axis=mybir.AxisListType.X, op=ALU.add)
        nc.vector.tensor_scalar_max(out=floored[:], in0=norm_sq[:], scalar1=1.0)
        nc.scalar.activation(out=norm_b[:], in_=floored[:], func=ACT.Sqrt, scale=float(P * P))
        nc.vector.reciprocal(out=c_over_b[:], in_=norm_b[:])

        def scale_round(n):
            if n % PERIOD in (0, 3):
                for h in range(ROUND):
                    cols = r_tiles[n][:, h * CHUNK : (h + 1) * CHUNK]
                    nc.scalar.activation(out=cols, in_=cols, func=ACT.Copy, scale=c_over_b[:])
            else:
                nc.gpsimd.tensor_scalar(
                    out=r_tiles[n][:],
                    in0=r_tiles[n][:],
                    scalar1=c_over_b[:],
                    scalar2=0.0,
                    op0=ALU.mult,
                    op1=ALU.add,
                )

        def sum_round(n):
            for h in range(ROUND):
                turned = xt_pool.tile([P, TILES_PER_BANK, P], F32, name="turned", tag="xt")
                for s in range(TILES_PER_BANK):
                    j = (h * TILES_PER_BANK + s) * P
                    nc.tensor.transpose(turned[:, s, :], r_tiles[n][:, j : j + P], ident[:])
                first = (n * ROUND + h) * TILES_PER_BANK
                if n % PERIOD == 2:
                    copied = stage.tile([P, TILES_PER_BANK, P], BF16, name="copied")
                    for s in range(TILES_PER_BANK):
                        nc.scalar.activation(
                            out=copied[:, s, :],
                            in_=turned[:, s, :],
                            func=ACT.Copy,
                            accum_out=out_cols[:, first + s : first + s + 1],
                        )
                else:
                    nc.vector.tensor_reduce(
                        out=out_cols[:, first : first + TILES_PER_BANK],
                        in_=turned[:],
                        axis=mybir.AxisListType.X,
                        op=ALU.add,
                    )

        for n in range(LEAD):
            scale_round(n)
        for n in range(n_rounds):
            if n + LEAD < n_rounds:
                scale_round(n + LEAD)
            sum_round(n)

        flipped = acc_pool.tile([P, CHUNK], F32, name="flipped", tag="acc")
        for h in range(2):
            nc.tensor.transpose(flipped[:, h * P : (h + 1) * P], out_cols[:, h * P : (h + 1) * P], ident[:])
        nc.vector.tensor_copy(out=out_rows[:], in_=flipped[:, 0 : 2 * P])
        out_2d = out.rearrange("(m j) -> m j", j=P)
        nc.sync.dma_start(out=out_2d[0:P, :], in_=out_rows[:, 0:P])
        nc.scalar.dma_start(out=out_2d[P:n_col_tiles, :], in_=out_rows[0 : n_col_tiles - P, P : 2 * P])
